import numpy as np
import ml_dtypes


def mxq(x, axis, fmt="e4m3"):
    dtype, down = {"e4m3": (ml_dtypes.float8_e4m3fn, 7), "e5m2": (ml_dtypes.float8_e5m2, 14)}[fmt]
    v = np.moveaxis(np.asarray(x, np.float32).astype(ml_dtypes.bfloat16).astype(np.float64), axis, -1)
    blocks = v.reshape(v.shape[:-1] + (-1, 32))
    amax = np.abs(blocks).max(-1, keepdims=True)
    byte = np.maximum(np.where(amax > 0, np.frexp(amax)[1] - 1 + 127, 0) - down, 1)
    scale = np.exp2(byte - 127.0)
    codes = (blocks / scale).astype(np.float32).astype(dtype).astype(np.float64)
    return np.moveaxis((codes * scale).reshape(v.shape), -1, axis)


WIDE = False


def mx_kscale(k):
    if not WIDE:
        return np.ones(k)
    levels = np.array([10, -10, 5, -5, 0])
    if k % 512:
        return np.exp2(np.random.permutation(np.resize(levels, k // 32))).repeat(32)
    a = np.empty((k // 512, 16))
    for p in range(k // 512):
        a[p, :8] = np.random.permutation(np.resize(levels, 8))
        for g in range(8):
            far = levels[np.abs(levels - a[p, g]) >= 10]
            a[p, g + 8] = far[np.random.randint(len(far))]
    return np.exp2(a.ravel()).repeat(32)


BF16 = ml_dtypes.bfloat16


def bf(x):
    return np.asarray(x, np.float32).astype(BF16)


def f64(x):
    return np.asarray(x).astype(np.float64)


E2M1 = np.array([0.0, 0.5, 1.0, 1.5, 2.0, 3.0, 4.0, 6.0, -0.0, -0.5, -1.0, -1.5, -2.0, -3.0, -4.0, -6.0])


def pack_weight(w, fmt):
    k, n = w.shape
    w = f64(bf(w)).reshape(k // 32, 32, n)
    amax = np.abs(w).max(1)
    if fmt == "e4m3":
        byte = np.frexp(amax)[1] - 1 + 127 - 7
    else:
        mant, ex = np.frexp(amax / 6.0)
        byte = np.where(mant > 0.5, ex, ex - 1) + 127
    byte = np.clip(np.where(amax > 0, byte, 1), 1, 254)
    scaled = (w * np.exp2(127.0 - byte)[:, None, :]).reshape(k, n).astype(np.float32)
    by_word = np.ascontiguousarray(scaled.reshape(k // 512, 128, 4, n).transpose(0, 1, 3, 2))
    if fmt == "e4m3":
        words = by_word.astype(ml_dtypes.float8_e4m3fn).view(np.uint8)
    else:
        c = by_word.astype(ml_dtypes.float4_e2m1fn).view(np.uint8) & 0xF
        words = c[..., 0::2] | (c[..., 1::2] << 4)
    return np.ascontiguousarray(words), np.ascontiguousarray(byte.astype(np.uint8).reshape(k // 512, 16, n))


def unpack_weight(words, scales, fmt):
    g, p, n, _ = words.shape
    if fmt == "e4m3":
        vals = np.ascontiguousarray(words).view(ml_dtypes.float8_e4m3fn).astype(np.float64)
    else:
        nib = np.empty((g, p, n, 4), np.uint8)
        nib[..., 0::2] = words & 0xF
        nib[..., 1::2] = words >> 4
        vals = E2M1[nib]
    vals = vals * np.repeat(np.exp2(scales.astype(np.float64) - 127.0), 8, axis=1)[..., None]
    return vals.transpose(0, 1, 3, 2).reshape(g * 512, n)


B, S, U, G, G2, N = 640, 10, 40, 512, 1024, 128


def draw0():
    s, t = mx_kscale(G), mx_kscale(G2)
    e = np.exp(np.random.standard_normal((B, S)))
    g1 = bf(np.maximum(np.random.standard_normal((B, S, G)), 0.0) * s)
    sW2 = np.random.standard_normal((G2, G)) * np.sqrt(2.0 / G) / s * t[:, None]
    sW2_words, sW2_scales = pack_weight(sW2.T, "e4m3")
    sb2 = bf(np.random.standard_normal(G2) * 0.3 * t)
    sW3 = np.random.standard_normal((N, G2)) * 1.5 * np.sqrt(2.0 / G2) / t
    sW3_words, sW3_scales = pack_weight(sW3.T, "e4m3")
    return {"g1": g1,
            "iab": bf(e / e.sum(1, keepdims=True)),
            "sW2_words": sW2_words,
            "sW2_scales": sW2_scales,
            "sb2": sb2,
            "sW3_words": sW3_words,
            "sW3_scales": sW3_scales,
            "sb3": bf(np.random.standard_normal(N) * 0.5)}


def core(g1, iab, sW2_words, sW2_scales, sb2, sW3_words, sW3_scales, sb3):
    h = np.maximum((mxq(f64(g1), 2, "e4m3") @ unpack_weight(sW2_words, sW2_scales, "e4m3")) + f64(sb2), 0.0)
    z = (mxq(h, 2, "e4m3") @ unpack_weight(sW3_words, sW3_scales, "e4m3")) + f64(sb3)
    e = np.exp(z - z.max(-1, keepdims=True))
    return e / e.sum(-1, keepdims=True) * f64(iab)[:, :, None]


def e4m3fn_bytes(y):
    return np.clip(np.asarray(y, np.float64), -448.0, 448.0).astype(np.float32).astype(ml_dtypes.float8_e4m3fn).view(np.uint8)


def e4m3fn_values(b):
    return np.asarray(b, np.uint8).view(ml_dtypes.float8_e4m3fn).astype(np.float64)


def setup_inputs():
    d = draw0()
    x0 = np.asarray(d['g1']).astype(np.float64)
    s = (np.max(np.abs(x0), axis=(0, 1), keepdims=True) / 448.0).astype(np.float32)
    out = {}
    for k, v in d.items():
        if k == 'g1':
            out['g1_bytes'] = e4m3fn_bytes(x0 / s.astype(np.float64))
            out['g1_scale'] = s
        else:
            out[k] = v
    return out


def reference(g1_bytes, g1_scale, iab, sW2_words, sW2_scales, sb2, sW3_words, sW3_scales, sb3):
    return core(e4m3fn_values(g1_bytes) * g1_scale.astype(np.float64), iab, sW2_words, sW2_scales, sb2, sW3_words, sW3_scales, sb3)

@@ -1,0 +1,344 @@
+import concourse.mybir as mybir
+from concourse.masks import make_identity
+from contextlib import ExitStack
+
+F32 = mybir.dt.float32
+BF16 = mybir.dt.bfloat16
+I32 = mybir.dt.int32
+U32 = mybir.dt.uint32
+U8 = mybir.dt.uint8
+FP8 = mybir.dt.float8_e4m3fn
+FP8X4 = mybir.dt.float8_e4m3fn_x4
+ACT = mybir.ActivationFunctionType
+ALU = mybir.AluOpType
+AX = mybir.AxisListType
+
+B, S, K1, K2, N = 640, 10, 512, 1024, 128
+TOKENS = B * S
+FLOPS = 2 * TOKENS * K1 * K2 + 2 * TOKENS * K2 * N
+
+P = 128
+ROWS = TOKENS // P
+SIZES = [2] + [4] * 11 + [2, 2]
+
+
+def tile_resourceallocationnetwork_pa_t_w8_kernel(
+    tc, g1_bytes, g1_scale, iab, sW2_words, sW2_scales, sb2, sW3_words, sW3_scales, sb3, out
+):
+    nc = tc.nc
+    chunks = len(SIZES)
+    first = [sum(SIZES[:c]) for c in range(chunks)]
+    g1_v = g1_bytes.rearrange("b s k -> (b s) k").rearrange("(p j) k -> p j k", j=ROWS)
+    out_v = out.rearrange("b s n -> (b s) n").rearrange("(p j) n -> p j n", j=ROWS)
+
+    with ExitStack() as ctx:
+        keep = ctx.enter_context(tc.tile_pool(name="keep", bufs=1))
+        two = ctx.enter_context(tc.tile_pool(name="two", bufs=2))
+        three = ctx.enter_context(tc.tile_pool(name="three", bufs=3))
+        four = ctx.enter_context(tc.tile_pool(name="four", bufs=4))
+        turn_ps = ctx.enter_context(tc.psum_pool(name="turn_ps", bufs=2))
+        h_ps = ctx.enter_context(tc.psum_pool(name="h_ps", bufs=4))
+        zt_ps = ctx.enter_context(tc.psum_pool(name="zt_ps", bufs=1))
+        z_ps = ctx.enter_context(tc.psum_pool(name="z_ps", bufs=1))
+
+        raw = [
+            keep.tile([P, SIZES[c], K1], U8, name="raw_%d" % c, align_bytes=64) for c in range(chunks)
+        ]
+        scale = keep.tile([P, 4, K1], F32, name="scale", align_bytes=64)
+        w2_raw = keep.tile([P, K2], I32, name="w2_raw", align_bytes=64)
+        w2 = keep.tile([P, 2, 4, P], I32, name="w2", align_bytes=64)
+        w2s_raw = keep.tile([P, K2], U8, name="w2s_raw", align_bytes=64)
+        w2s = keep.tile([P, 2, 4, P], U8, name="w2s", align_bytes=64)
+        w3 = keep.tile([P, 2, N], I32, name="w3", align_bytes=64)
+        w3s = keep.tile([P, 2, N], U8, name="w3s", align_bytes=64)
+        b2 = keep.tile([P, 2, 4], BF16, name="b2")
+        b3 = keep.tile([P, 1], BF16, name="b3")
+        iab_raw = keep.tile([P, ROWS], BF16, name="iab_raw")
+        share = keep.tile([P, ROWS], F32, name="share")
+        ident = keep.tile([P, P], F32, name="ident", align_bytes=64)
+        warm = keep.tile([P, 1], F32, name="warm")
+
+        ctx.enter_context(tc.manual_schedule())
+
+        def load(c):
+            nc.sync.dma_start(out=raw[c][:], in_=g1_v[:, first[c] : first[c] + SIZES[c], :])
+
+        nc.vector.memset(w2s_raw[:].bitcast(I32), 0)
+        nc.vector.memset(w3s[:].rearrange("p g n -> p (g n)").bitcast(I32), 0)
+        nc.vector.memset(warm[:], 0.0)
+        nc.scalar.activation(out=warm[:], in_=warm[:], func=ACT.Exp)
+        make_identity(nc, ident[:])
+
+        load(0)
+        nc.sync.dma_start(
+            out=scale[:, 0, :], in_=g1_scale.rearrange("a b k -> (a b k)").partition_broadcast(P)
+        )
+        nc.sync.dma_start(
+            out=w2_raw[:], in_=sW2_words[0].rearrange("p n t -> p (n t)").bitcast(I32)
+        )
+        for q in range(4):
+            nc.sync.dma_start(
+                out=w2s_raw[32 * q : 32 * q + 4, :].bitcast(I32),
+                in_=sW2_scales[0, 4 * q : 4 * q + 4, :].bitcast(I32),
+            )
+        nc.scalar.dma_start(out=b2[:], in_=sb2.rearrange("(g p t) -> p g t", p=P, t=4))
+        nc.scalar.dma_start(out=b3[:], in_=sb3.rearrange("(n o) -> n o", o=1))
+        nc.scalar.dma_start(
+            out=iab_raw[:], in_=iab.rearrange("b s -> (b s)").rearrange("(p j) -> p j", j=ROWS)
+        )
+        load(1)
+        load(2)
+        for g in range(2):
+            nc.sync.dma_start(
+                out=w3[:, g, :], in_=sW3_words[g].rearrange("p n t -> p (n t)").bitcast(I32)
+            )
+        for q in range(4):
+            nc.sync.dma_start(
+                out=w3s[32 * q : 32 * q + 4, :, :].rearrange("p g n -> p g n").bitcast(I32),
+                in_=sW3_scales[:, 4 * q : 4 * q + 4, :].rearrange("g q n -> q g n").bitcast(I32),
+            )
+        for c in range(3, chunks):
+            load(c)
+
+        nc.gpsimd.tensor_copy(out=share[:], in_=iab_raw[:])
+
+        live = {}
+
+        def widen(c, half):
+            n = SIZES[c]
+            if half == 0:
+                live["x", c] = three.tile([P, 4, K1], BF16, name="x", align_bytes=64)
+            x = live["x", c]
+            if c == 0:
+                parts = [(half, half + 1)]
+            else:
+                parts = [(half * n // 2, (half + 1) * n // 2)]
+            for lo, hi in parts:
+                nc.vector.tensor_tensor(
+                    out=x[:, lo:hi, :],
+                    in0=raw[c][:, lo:hi, :].bitcast(FP8),
+                    in1=scale[:, 0 : hi - lo, :],
+                    op=ALU.mult,
+                )
+
+        def turn(c):
+            x = live["x", c]
+            live["turned", c] = []
+            for b in range(SIZES[c] // 2):
+                xt = turn_ps.tile([P, 2, 2, P], F32, name="xt")
+                for a in range(2):
+                    words = x[:, 2 * b + a, :].bitcast(F32)
+                    for u in range(2):
+                        nc.tensor.transpose(xt[:, a, u, :], words[:, u : 2 * P : 2], ident[:])
+                live["turned", c].append(xt)
+
+        def gather(c):
+            n = SIZES[c]
+            live["xg", c] = two.tile([P, 4 * P, 4], BF16, name="xg", align_bytes=64)
+            xg = live["xg", c]
+            words = xg[:].rearrange("p n t -> p (n t)").bitcast(F32)
+            for b in range(n // 2):
+                xt = live["turned", c][b]
+                nc.scalar.copy(
+                    out=words[:, 512 * b : 512 * (b + 1)].rearrange("p (a r u) -> p a r u", a=2, u=2),
+                    in_=xt[:].rearrange("p a u r -> p a r u"),
+                )
+
+        def quant_x(c):
+            n = SIZES[c]
+            codes = two.tile([P, 4 * P], U32, name="x_codes", align_bytes=64)
+            scales = two.tile([P, 4 * P], U8, name="x_scales", align_bytes=64)
+            live["xq", c] = (codes, scales)
+            nc.vector.quantize_mx(
+                out=codes[:, : n * P].bitcast(FP8X4),
+                scales=scales[:, : n * P],
+                in_=live["xg", c][:, : n * P, :].rearrange("p n t -> p (n t)"),
+            )
+
+        def layer1(c, g):
+            w = SIZES[c] * P
+            codes, scales = live["xq", c]
+            live["h", c, g] = []
+            for t in range(4):
+                acc = h_ps.tile([P, 4 * P], F32, name="acc")
+                nc.tensor.matmul_mx(
+                    out=acc[:, :w],
+                    lhsT=w2[:, g, t, :].bitcast(FP8X4),
+                    lhsT_scale=w2s[:, g, t, :],
+                    rhs=codes[:, :w].bitcast(FP8X4),
+                    rhs_scale=scales[:, :w],
+                    start=True,
+                    stop=True,
+                )
+                live["h", c, g].append(acc)
+
+        def relu(c, g, planes):
+            w = SIZES[c] * P
+            if planes[0] == 0:
+                live["hp", c, g] = three.tile([P, 4, 4 * P], BF16, name="hp", align_bytes=64)
+            hp = live["hp", c, g]
+            for t in planes:
+                nc.scalar.activation(
+                    out=hp[:, t, :w],
+                    in_=live["h", c, g][t][:, :w],
+                    func=ACT.Relu,
+                    bias=b2[:, g, t : t + 1],
+                )
+
+        def weave(c, g):
+            w = SIZES[c] * P
+            hg = three.tile([P, 4 * P, 4], BF16, name="hg", align_bytes=64)
+            live["hg", c, g] = hg
+            nc.vector.tensor_copy(
+                out=hg[:, :w, :].rearrange("p (c i) t -> p c t i", i=4),
+                in_=live["hp", c, g][:, :, :w].rearrange("p t (c i) -> p c t i", i=4),
+            )
+
+        def quant_h(c, g):
+            w = SIZES[c] * P
+            codes = four.tile([P, 4 * P], U32, name="h_codes", align_bytes=64)
+            scales = four.tile([P, 4 * P], U8, name="h_scales", align_bytes=64)
+            live["hq", c, g] = (codes, scales)
+            nc.vector.quantize_mx(
+                out=codes[:, :w].bitcast(FP8X4),
+                scales=scales[:, :w],
+                in_=live["hg", c, g][:, :w, :].rearrange("p n t -> p (n t)"),
+            )
+
+        def layer2(c):
+            w = SIZES[c] * P
+            zt = zt_ps.tile([P, 4 * P], F32, name="zt")
+            live["zt", c] = zt
+            for g in range(2):
+                codes, scales = live["hq", c, g]
+                nc.tensor.matmul_mx(
+                    out=zt[:, :w],
+                    lhsT=w3[:, g, :].bitcast(FP8X4),
+                    lhsT_scale=w3s[:, g, :],
+                    rhs=codes[:, :w].bitcast(FP8X4),
+                    rhs_scale=scales[:, :w],
+                    start=(g == 0),
+                    stop=(g == 1),
+                )
+
+        def add_b3(c):
+            w = SIZES[c] * P
+            zs = three.tile([P, 4 * P], F32, name="zs")
+            live["zs", c] = zs
+            nc.scalar.activation(
+                out=zs[:, :w], in_=live["zt", c][:, :w], func=ACT.Identity, bias=b3[:]
+            )
+
+        def turn_z(c):
+            z = z_ps.tile([P, 4, N], F32, name="z")
+            live["zb", c] = z
+            for a in range(SIZES[c]):
+                nc.tensor.transpose(z[:, a, :], live["zs", c][:, a * P : (a + 1) * P], ident[:])
+
+        def row_max(c):
+            n = SIZES[c]
+            nm = three.tile([P, 4], F32, name="nm")
+            live["nm", c] = nm
+            nc.vector.tensor_reduce(
+                out=nm[:, :n], in_=live["zb", c][:, :n, :], axis=AX.X, op=ALU.max, negate=True
+            )
+
+        def expo(c):
+            e = three.tile([P, 4, N], F32, name="e")
+            total = three.tile([P, 4], F32, name="total")
+            live["e", c] = (e, total)
+            for a in range(SIZES[c]):
+                nc.scalar.activation(
+                    out=e[:, a, :],
+                    in_=live["zb", c][:, a, :],
+                    func=ACT.Exp,
+                    bias=live["nm", c][:, a : a + 1],
+                    accum_out=total[:, a : a + 1],
+                )
+
+        def invert(c):
+            n = SIZES[c]
+            e, total = live["e", c]
+            inv = three.tile([P, 4], F32, name="inv")
+            live["inv", c] = inv
+            nc.vector.reciprocal(out=inv[:, :n], in_=total[:, :n])
+
+        def finish(c):
+            n = SIZES[c]
+            e, total = live["e", c]
+            res = three.tile([P, 4, N], F32, name="res")
+            for a in range(n):
+                j = first[c] + a
+                nc.vector.tensor_scalar(
+                    out=res[:, a, :],
+                    in0=e[:, a, :],
+                    scalar1=live["inv", c][:, a : a + 1],
+                    scalar2=share[:, j : j + 1],
+                    op0=ALU.mult,
+                    op1=ALU.mult,
+                )
+            nc.sync.dma_start(out=out_v[:, first[c] : first[c] + n, :], in_=res[:, :n, :])
+
+        def on(c):
+            return 0 <= c < chunks
+
+        widen(0, 0)
+        widen(0, 1)
+        for j in range(1, 4):
+            nc.scalar.copy(out=scale[:, j, :], in_=scale[:, 0, :])
+        turn(0)
+        gather(0)
+        for g in range(2):
+            nc.vector.tensor_copy(
+                out=w2[:, g, :, :],
+                in_=w2_raw[:, 4 * P * g : 4 * P * (g + 1)].rearrange("p (m t) -> p t m", t=4),
+            )
+            nc.vector.tensor_copy(
+                out=w2s[:, g, :, :],
+                in_=w2s_raw[:, 4 * P * g : 4 * P * (g + 1)].rearrange("p (m t) -> p t m", t=4),
+            )
+            if g == 0:
+                quant_x(0)
+        widen(1, 0)
+        widen(1, 1)
+
+        for i in range(chunks + 4):
+            if on(i):
+                layer1(i, 0)
+                relu(i, 0, range(4))
+            if on(i + 1):
+                turn(i + 1)
+                gather(i + 1)
+            if on(i - 2):
+                turn_z(i - 2)
+            if on(i - 3):
+                invert(i - 3)
+            if on(i - 1):
+                weave(i - 1, 1)
+            if on(i - 3):
+                finish(i - 3)
+            if on(i - 1):
+                quant_h(i - 1, 1)
+            if on(i):
+                layer1(i, 1)
+            if on(i - 1):
+                layer2(i - 1)
+            if on(i):
+                relu(i, 1, range(2))
+            if on(i - 1):
+                add_b3(i - 1)
+            if on(i):
+                relu(i, 1, range(2, 4))
+            if on(i + 2):
+                widen(i + 2, 0)
+            if on(i):
+                weave(i, 0)
+            if on(i + 1):
+                quant_x(i + 1)
+            if on(i - 2):
+                row_max(i - 2)
+                expo(i - 2)
+            if on(i + 2):
+                widen(i + 2, 1)
+            if on(i):
+                quant_h(i, 0)

@@ -19,7 +19,8 @@ FLOPS = 2 * TOKENS * K1 * K2 + 2 * TOKENS * K2 * N
 
 P = 128
 ROWS = TOKENS // P
-SIZES = [2] + [4] * 11 + [2, 2]
+SIZES = [2] + [4] * 11 + [2, 1, 1]
+DIRECT = []
 
 
 def tile_resourceallocationnetwork_pa_t_w8_kernel(
@@ -44,7 +45,7 @@ def tile_resourceallocationnetwork_pa_t_w8_kernel(
         raw = [
             keep.tile([P, SIZES[c], K1], U8, name="raw_%d" % c, align_bytes=64) for c in range(chunks)
         ]
-        scale = keep.tile([P, 4, K1], F32, name="scale", align_bytes=64)
+        scale = keep.tile([P, 4], F32, name="scale")
         w2_raw = keep.tile([P, K2], I32, name="w2_raw", align_bytes=64)
         w2 = keep.tile([P, 2, 4, P], I32, name="w2", align_bytes=64)
         w2s_raw = keep.tile([P, K2], U8, name="w2s_raw", align_bytes=64)
@@ -53,6 +54,8 @@ def tile_resourceallocationnetwork_pa_t_w8_kernel(
         w3s = keep.tile([P, 2, N], U8, name="w3s", align_bytes=64)
         b2 = keep.tile([P, 2, 4], BF16, name="b2")
         b3 = keep.tile([P, 1], BF16, name="b3")
+        b3_row = keep.tile([P, N], BF16, name="b3_row")
+        b3_rows = keep.tile([P, 4, N], F32, name="b3_rows")
         iab_raw = keep.tile([P, ROWS], BF16, name="iab_raw")
         share = keep.tile([P, ROWS], F32, name="share")
         ident = keep.tile([P, P], F32, name="ident", align_bytes=64)
@@ -70,9 +73,8 @@ def tile_resourceallocationnetwork_pa_t_w8_kernel(
         make_identity(nc, ident[:])
 
         load(0)
-        nc.sync.dma_start(
-            out=scale[:, 0, :], in_=g1_scale.rearrange("a b k -> (a b k)").partition_broadcast(P)
-        )
+        nc.sync.dma_start(out=scale[:], in_=g1_scale.rearrange("a b (p t) -> p (a b t)", t=4))
+        load(1)
         nc.sync.dma_start(
             out=w2_raw[:], in_=sW2_words[0].rearrange("p n t -> p (n t)").bitcast(I32)
         )
@@ -81,12 +83,12 @@ def tile_resourceallocationnetwork_pa_t_w8_kernel(
                 out=w2s_raw[32 * q : 32 * q + 4, :].bitcast(I32),
                 in_=sW2_scales[0, 4 * q : 4 * q + 4, :].bitcast(I32),
             )
-        nc.scalar.dma_start(out=b2[:], in_=sb2.rearrange("(g p t) -> p g t", p=P, t=4))
-        nc.scalar.dma_start(out=b3[:], in_=sb3.rearrange("(n o) -> n o", o=1))
-        nc.scalar.dma_start(
+        nc.gpsimd.dma_start(out=b2[:], in_=sb2.rearrange("(g p t) -> p g t", p=P, t=4))
+        nc.gpsimd.dma_start(out=b3_row[:], in_=sb3.partition_broadcast(P))
+        nc.gpsimd.dma_start(out=b3[:], in_=sb3.rearrange("(n o) -> n o", o=1))
+        nc.gpsimd.dma_start(
             out=iab_raw[:], in_=iab.rearrange("b s -> (b s)").rearrange("(p j) -> p j", j=ROWS)
         )
-        load(1)
         load(2)
         for g in range(2):
             nc.sync.dma_start(
@@ -100,7 +102,6 @@ def tile_resourceallocationnetwork_pa_t_w8_kernel(
         for c in range(3, chunks):
             load(c)
 
-        nc.gpsimd.tensor_copy(out=share[:], in_=iab_raw[:])
 
         live = {}
 
@@ -109,40 +110,36 @@ def tile_resourceallocationnetwork_pa_t_w8_kernel(
             if half == 0:
                 live["x", c] = three.tile([P, 4, K1], BF16, name="x", align_bytes=64)
             x = live["x", c]
-            if c == 0:
-                parts = [(half, half + 1)]
-            else:
-                parts = [(half * n // 2, (half + 1) * n // 2)]
-            for lo, hi in parts:
-                nc.vector.tensor_tensor(
-                    out=x[:, lo:hi, :],
-                    in0=raw[c][:, lo:hi, :].bitcast(FP8),
-                    in1=scale[:, 0 : hi - lo, :],
-                    op=ALU.mult,
-                )
+            lo, hi = (half * n + 1) // 2, ((half + 1) * n + 1) // 2
+            if lo < hi:
+                nc.scalar.copy(out=x[:, lo:hi, :], in_=raw[c][:, lo:hi, :].bitcast(FP8))
 
-        def turn(c):
+        def turn(c, b):
             x = live["x", c]
-            live["turned", c] = []
-            for b in range(SIZES[c] // 2):
-                xt = turn_ps.tile([P, 2, 2, P], F32, name="xt")
-                for a in range(2):
-                    words = x[:, 2 * b + a, :].bitcast(F32)
-                    for u in range(2):
-                        nc.tensor.transpose(xt[:, a, u, :], words[:, u : 2 * P : 2], ident[:])
-                live["turned", c].append(xt)
+            xt = turn_ps.tile([P, 2, 2, P], F32, name="xt")
+            for a in range(min(2, SIZES[c] - 2 * b)):
+                words = x[:, 2 * b + a, :].bitcast(F32)
+                for u in range(2):
+                    nc.tensor.transpose(xt[:, u, a, :], words[:, u : 2 * P : 2], ident[:])
+            live["turned", c, b] = xt
 
-        def gather(c):
-            n = SIZES[c]
-            live["xg", c] = two.tile([P, 4 * P, 4], BF16, name="xg", align_bytes=64)
+        def gather(c, b):
+            m = min(2, SIZES[c] - 2 * b)
+            if b == 0:
+                live["xg", c] = two.tile([P, 4 * P, 4], BF16, name="xg", align_bytes=64)
             xg = live["xg", c]
-            words = xg[:].rearrange("p n t -> p (n t)").bitcast(F32)
-            for b in range(n // 2):
-                xt = live["turned", c][b]
-                nc.scalar.copy(
-                    out=words[:, 512 * b : 512 * (b + 1)].rearrange("p (a r u) -> p a r u", a=2, u=2),
-                    in_=xt[:].rearrange("p a u r -> p a r u"),
-                )
+            xt = live["turned", c, b]
+            nc.vector.tensor_tensor(
+                out=xg[:, 2 * P * b : 2 * P * b + m * P, :].rearrange("p n (u e) -> p n u e", e=2),
+                in0=xt[:]
+                .rearrange("p u a r -> p u (a r)")
+                .bitcast(BF16)[:, :, : 2 * P * m]
+                .rearrange("p u (n e) -> p n u e", e=2),
+                in1=scale[:]
+                .rearrange("p (o u e) -> p o u e", o=1, e=2)
+                .to_broadcast([P, m * P, 2, 2]),
+                op=ALU.mult,
+            )
 
         def quant_x(c):
             n = SIZES[c]
@@ -207,6 +204,23 @@ def tile_resourceallocationnetwork_pa_t_w8_kernel(
 
         def layer2(c):
             w = SIZES[c] * P
+            if c in DIRECT:
+                z = z_ps.tile([P, 4, N], F32, name="z")
+                live["zt", c] = z
+                for a in range(SIZES[c]):
+                    cols = slice(a * P, (a + 1) * P)
+                    for g in range(2):
+                        codes, scales = live["hq", c, g]
+                        nc.tensor.matmul_mx(
+                            out=z[:, a, :],
+                            lhsT=codes[:, cols].bitcast(FP8X4),
+                            lhsT_scale=scales[:, cols],
+                            rhs=w3[:, g, :].bitcast(FP8X4),
+                            rhs_scale=w3s[:, g, :],
+                            start=(g == 0),
+                            stop=(g == 1),
+                        )
+                return
             zt = zt_ps.tile([P, 4 * P], F32, name="zt")
             live["zt", c] = zt
             for g in range(2):
@@ -223,6 +237,14 @@ def tile_resourceallocationnetwork_pa_t_w8_kernel(
 
         def add_b3(c):
             w = SIZES[c] * P
+            if c in DIRECT:
+                n = SIZES[c]
+                zb = three.tile([P, 4, N], F32, name="zb")
+                live["zb", c] = zb
+                nc.vector.tensor_tensor(
+                    out=zb[:, :n, :], in0=live["zt", c][:, :n, :], in1=b3_rows[:, :n, :], op=ALU.add
+                )
+                return
             zs = three.tile([P, 4 * P], F32, name="zs")
             live["zs", c] = zs
             nc.scalar.activation(
@@ -230,6 +252,8 @@ def tile_resourceallocationnetwork_pa_t_w8_kernel(
             )
 
         def turn_z(c):
+            if c in DIRECT:
+                return
             z = z_ps.tile([P, 4, N], F32, name="z")
             live["zb", c] = z
             for a in range(SIZES[c]):
@@ -282,63 +306,97 @@ def tile_resourceallocationnetwork_pa_t_w8_kernel(
         def on(c):
             return 0 <= c < chunks
 
-        widen(0, 0)
-        widen(0, 1)
-        for j in range(1, 4):
-            nc.scalar.copy(out=scale[:, j, :], in_=scale[:, 0, :])
-        turn(0)
-        gather(0)
-        for g in range(2):
-            nc.vector.tensor_copy(
-                out=w2[:, g, :, :],
-                in_=w2_raw[:, 4 * P * g : 4 * P * (g + 1)].rearrange("p (m t) -> p t m", t=4),
-            )
-            nc.vector.tensor_copy(
-                out=w2s[:, g, :, :],
-                in_=w2s_raw[:, 4 * P * g : 4 * P * (g + 1)].rearrange("p (m t) -> p t m", t=4),
-            )
-            if g == 0:
-                quant_x(0)
-        widen(1, 0)
-        widen(1, 1)
+        done = {}
 
+        def need(*keys):
+            for k in keys:
+                assert k in done, k
+
+        def mark(k):
+            done[k] = True
+
+        def do(name, c, *a):
+            if not on(c):
+                return
+            if name == "W":
+                widen(c, a[0])
+            elif name == "T":
+                if 2 * a[0] >= SIZES[c]:
+                    mark((name, c) + tuple(a))
+                    return
+                need(("W", c, 0), ("W", c, 1))
+                turn(c, a[0])
+            elif name == "G":
+                if 2 * a[0] >= SIZES[c]:
+                    mark((name, c) + tuple(a))
+                    return
+                need(("T", c, a[0]))
+                gather(c, a[0])
+            elif name == "X":
+                need(("G", c, 0), ("G", c, 1))
+                quant_x(c)
+            elif name == "L":
+                need(("X", c), ("p", 0, a[0]), ("q", 0, a[0]))
+                layer1(c, a[0])
+            elif name == "R":
+                need(("L", c, a[0]))
+                relu(c, a[0], [a[1]])
+            elif name == "V":
+                need(*[("R", c, a[0], t) for t in range(4)])
+                weave(c, a[0])
+            elif name == "Q":
+                need(("V", c, a[0]))
+                quant_h(c, a[0])
+            elif name == "M":
+                need(("Q", c, 0), ("Q", c, 1))
+                layer2(c)
+            elif name == "D":
+                if c not in DIRECT:
+                    return
+                need(("M", c))
+                add_b3(c)
+                mark(("B", c))
+                mark(("Z", c))
+            elif name in ("B", "Z") and c in DIRECT:
+                return
+            elif name == "p":
+                g = a[0]
+                nc.vector.tensor_copy(
+                    out=w2[:, g, :, :],
+                    in_=w2_raw[:, 4 * P * g : 4 * P * (g + 1)].rearrange("p (m t) -> p t m", t=4),
+                )
+            elif name == "q":
+                g = a[0]
+                (nc.vector if g == 0 else nc.gpsimd).tensor_copy(
+                    out=w2s[:, g, :, :],
+                    in_=w2s_raw[:, 4 * P * g : 4 * P * (g + 1)].rearrange("p (m t) -> p t m", t=4),
+                )
+            elif name == "B":
+                need(("M", c))
+                add_b3(c)
+            elif name == "Z":
+                need(("B", c))
+                turn_z(c)
+            elif name == "A":
+                need(("Z", c))
+                row_max(c)
+            elif name == "E":
+                need(("A", c))
+                expo(c)
+            elif name == "I":
+                need(("E", c))
+                invert(c)
+            elif name == "F":
+                need(("I", c))
+                finish(c)
+            mark((name, c) + tuple(a))
+
+        for name, c, *a in [["W", 0, 0], ["W", 0, 1], ["T", 0, 0], ["W", 1, 0], ["T", 0, 1], ["W", 1, 1], ["G", 0, 0], ["G", 0, 1], ["p", 0, 0], ["T", 1, 1], ["W", 2, 0], ["q", 0, 0], ["p", 0, 1], ["X", 0], ["T", 1, 0], ["L", 0, 0], ["G", 1, 0], ["q", 0, 1], ["R", 0, 0, 0], ["R", 0, 0, 1], ["R", 0, 0, 3], ["G", 1, 1], ["R", 0, 0, 2], ["W", 2, 1], ["X", 1], ["L", 0, 1], ["R", 0, 1, 0], ["R", 0, 1, 1], ["R", 0, 1, 2], ["R", 0, 1, 3]]:
+            do(name, c, *a)
+        nc.gpsimd.tensor_copy(out=share[:], in_=iab_raw[:])
+        for a in range(4):
+            nc.gpsimd.tensor_copy(out=b3_rows[:, a, :], in_=b3_row[:])
         for i in range(chunks + 4):
-            if on(i):
-                layer1(i, 0)
-                relu(i, 0, range(4))
-            if on(i + 1):
-                turn(i + 1)
-                gather(i + 1)
-            if on(i - 2):
-                turn_z(i - 2)
-            if on(i - 3):
-                invert(i - 3)
-            if on(i - 1):
-                weave(i - 1, 1)
-            if on(i - 3):
-                finish(i - 3)
-            if on(i - 1):
-                quant_h(i - 1, 1)
-            if on(i):
-                layer1(i, 1)
-            if on(i - 1):
-                layer2(i - 1)
-            if on(i):
-                relu(i, 1, range(2))
-            if on(i - 1):
-                add_b3(i - 1)
-            if on(i):
-                relu(i, 1, range(2, 4))
-            if on(i + 2):
-                widen(i + 2, 0)
-            if on(i):
-                weave(i, 0)
-            if on(i + 1):
-                quant_x(i + 1)
-            if on(i - 2):
-                row_max(i - 2)
-                expo(i - 2)
-            if on(i + 2):
-                widen(i + 2, 1)
-            if on(i):
-                quant_h(i, 0)
+            for name, off, *a in [["T", 1, 0], ["V", -1, 1], ["G", 1, 0], ["L", 0, 0], ["R", 0, 0, 0], ["D", -1], ["Q", -1, 1], ["T", 1, 1], ["R", 0, 0, 2], ["Z", -2], ["G", 1, 1], ["R", 0, 0, 1], ["W", 2, 0], ["A", -2], ["I", -3], ["R", 0, 0, 3], ["L", 0, 1], ["M", -1], ["R", 0, 1, 0], ["R", 0, 1, 1], ["R", 0, 1, 3], ["R", 0, 1, 2], ["V", 0, 0], ["B", -1], ["W", 2, 1], ["X", 1], ["F", -3], ["Q", 0, 0], ["E", -2]]:
+                if (name, i + off) + tuple(a) not in done:
+                    do(name, i + off, *a)

@@ -19,8 +19,9 @@ FLOPS = 2 * TOKENS * K1 * K2 + 2 * TOKENS * K2 * N
 
 P = 128
 ROWS = TOKENS // P
-SIZES = [2] + [4] * 11 + [2, 1, 1]
-DIRECT = []
+SIZES = [1, 2] + [4] * 11 + [2, 1]
+DIRECT = [2, 4, 5, 7, 8, 10, 11]
+POOL = [224, 224]
 
 
 def tile_resourceallocationnetwork_pa_t_w8_kernel(
@@ -36,6 +37,7 @@ def tile_resourceallocationnetwork_pa_t_w8_kernel(
         keep = ctx.enter_context(tc.tile_pool(name="keep", bufs=1))
         two = ctx.enter_context(tc.tile_pool(name="two", bufs=2))
         three = ctx.enter_context(tc.tile_pool(name="three", bufs=3))
+        five = ctx.enter_context(tc.tile_pool(name="five", bufs=5))
         four = ctx.enter_context(tc.tile_pool(name="four", bufs=4))
         turn_ps = ctx.enter_context(tc.psum_pool(name="turn_ps", bufs=2))
         h_ps = ctx.enter_context(tc.psum_pool(name="h_ps", bufs=4))
@@ -172,7 +174,7 @@ def tile_resourceallocationnetwork_pa_t_w8_kernel(
         def relu(c, g, planes):
             w = SIZES[c] * P
             if planes[0] == 0:
-                live["hp", c, g] = three.tile([P, 4, 4 * P], BF16, name="hp", align_bytes=64)
+                live["hp", c, g] = five.tile([P, 4, 4 * P], BF16, name="hp", align_bytes=64)
             hp = live["hp", c, g]
             for t in planes:
                 nc.scalar.activation(
@@ -182,14 +184,37 @@ def tile_resourceallocationnetwork_pa_t_w8_kernel(
                     bias=b2[:, g, t : t + 1],
                 )
 
+        def pooled(c, g):
+            return POOL[g] if SIZES[c] == 4 and c >= 2 else 0
+
+        def tile_hg(c, g):
+            if ("hg", c, g) not in live:
+                live["hg", c, g] = two.tile([P, 4 * P, 4], BF16, name="hg", align_bytes=64)
+            return live["hg", c, g]
+
         def weave(c, g):
             w = SIZES[c] * P
-            hg = three.tile([P, 4 * P, 4], BF16, name="hg", align_bytes=64)
-            live["hg", c, g] = hg
-            nc.vector.tensor_copy(
-                out=hg[:, :w, :].rearrange("p (c i) t -> p c t i", i=4),
-                in_=live["hp", c, g][:, :, :w].rearrange("p t (c i) -> p c t i", i=4),
-            )
+            hg = tile_hg(c, g)
+            w -= pooled(c, g)
+            if w:
+                nc.vector.tensor_copy(
+                    out=hg[:, :w, :].rearrange("p (c i) t -> p c t i", i=4),
+                    in_=live["hp", c, g][:, :, :w].rearrange("p t (c i) -> p c t i", i=4),
+                )
+
+        def pool_weave(c, g):
+            w = SIZES[c] * P
+            k = pooled(c, g)
+            if k:
+                hg = tile_hg(c, g)
+                nc.gpsimd.tensor_scalar(
+                    out=hg[:, w - k : w, :],
+                    in0=live["hp", c, g][:, :, w - k : w].rearrange("p t n -> p n t"),
+                    scalar1=1.0,
+                    scalar2=0.0,
+                    op0=ALU.mult,
+                    op1=ALU.add,
+                )
 
         def quant_h(c, g):
             w = SIZES[c] * P
@@ -205,7 +230,7 @@ def tile_resourceallocationnetwork_pa_t_w8_kernel(
         def layer2(c):
             w = SIZES[c] * P
             if c in DIRECT:
-                z = z_ps.tile([P, 4, N], F32, name="z")
+                z = zt_ps.tile([P, 4 * P], F32, name="zt").rearrange("p (a n) -> p a n", a=4)
                 live["zt", c] = z
                 for a in range(SIZES[c]):
                     cols = slice(a * P, (a + 1) * P)
@@ -239,13 +264,13 @@ def tile_resourceallocationnetwork_pa_t_w8_kernel(
             w = SIZES[c] * P
             if c in DIRECT:
                 n = SIZES[c]
-                zb = three.tile([P, 4, N], F32, name="zb")
+                zb = four.tile([P, 4, N], F32, name="zb")
                 live["zb", c] = zb
                 nc.vector.tensor_tensor(
                     out=zb[:, :n, :], in0=live["zt", c][:, :n, :], in1=b3_rows[:, :n, :], op=ALU.add
                 )
                 return
-            zs = three.tile([P, 4 * P], F32, name="zs")
+            zs = four.tile([P, 4 * P], F32, name="zs")
             live["zs", c] = zs
             nc.scalar.activation(
                 out=zs[:, :w], in_=live["zt", c][:, :w], func=ACT.Identity, bias=b3[:]
@@ -261,15 +286,15 @@ def tile_resourceallocationnetwork_pa_t_w8_kernel(
 
         def row_max(c):
             n = SIZES[c]
-            nm = three.tile([P, 4], F32, name="nm")
+            nm = four.tile([P, 4], F32, name="nm")
             live["nm", c] = nm
             nc.vector.tensor_reduce(
                 out=nm[:, :n], in_=live["zb", c][:, :n, :], axis=AX.X, op=ALU.max, negate=True
             )
 
         def expo(c):
-            e = three.tile([P, 4, N], F32, name="e")
-            total = three.tile([P, 4], F32, name="total")
+            e = four.tile([P, 4, N], F32, name="e")
+            total = four.tile([P, 4], F32, name="total")
             live["e", c] = (e, total)
             for a in range(SIZES[c]):
                 nc.scalar.activation(
@@ -283,7 +308,7 @@ def tile_resourceallocationnetwork_pa_t_w8_kernel(
         def invert(c):
             n = SIZES[c]
             e, total = live["e", c]
-            inv = three.tile([P, 4], F32, name="inv")
+            inv = four.tile([P, 4], F32, name="inv")
             live["inv", c] = inv
             nc.vector.reciprocal(out=inv[:, :n], in_=total[:, :n])
 
@@ -344,8 +369,11 @@ def tile_resourceallocationnetwork_pa_t_w8_kernel(
             elif name == "V":
                 need(*[("R", c, a[0], t) for t in range(4)])
                 weave(c, a[0])
+            elif name == "P":
+                need(*[("R", c, a[0], t) for t in range(4)])
+                pool_weave(c, a[0])
             elif name == "Q":
-                need(("V", c, a[0]))
+                need(("V", c, a[0]), ("P", c, a[0]))
                 quant_h(c, a[0])
             elif name == "M":
                 need(("Q", c, 0), ("Q", c, 1))
@@ -391,12 +419,12 @@ def tile_resourceallocationnetwork_pa_t_w8_kernel(
                 finish(c)
             mark((name, c) + tuple(a))
 
-        for name, c, *a in [["W", 0, 0], ["W", 0, 1], ["T", 0, 0], ["W", 1, 0], ["T", 0, 1], ["W", 1, 1], ["G", 0, 0], ["G", 0, 1], ["p", 0, 0], ["T", 1, 1], ["W", 2, 0], ["q", 0, 0], ["p", 0, 1], ["X", 0], ["T", 1, 0], ["L", 0, 0], ["G", 1, 0], ["q", 0, 1], ["R", 0, 0, 0], ["R", 0, 0, 1], ["R", 0, 0, 3], ["G", 1, 1], ["R", 0, 0, 2], ["W", 2, 1], ["X", 1], ["L", 0, 1], ["R", 0, 1, 0], ["R", 0, 1, 1], ["R", 0, 1, 2], ["R", 0, 1, 3]]:
+        for name, c, *a in [["W", 0, 0], ["G", 0, 1], ["W", 1, 0], ["W", 0, 1], ["T", 0, 0], ["W", 1, 1], ["G", 0, 0], ["W", 2, 0], ["p", 0, 0], ["X", 0], ["T", 1, 0], ["q", 0, 0], ["G", 1, 0], ["p", 0, 1], ["q", 0, 1], ["G", 1, 1], ["T", 0, 1], ["L", 0, 0], ["W", 2, 1], ["X", 1], ["R", 0, 0, 0], ["R", 0, 0, 2], ["R", 0, 0, 3], ["R", 0, 0, 1], ["L", 0, 1], ["R", 0, 1, 0], ["T", 1, 1], ["R", 0, 1, 1], ["R", 0, 1, 2], ["R", 0, 1, 3]]:
             do(name, c, *a)
         nc.gpsimd.tensor_copy(out=share[:], in_=iab_raw[:])
         for a in range(4):
             nc.gpsimd.tensor_copy(out=b3_rows[:, a, :], in_=b3_row[:])
-        for i in range(chunks + 4):
-            for name, off, *a in [["T", 1, 0], ["V", -1, 1], ["G", 1, 0], ["L", 0, 0], ["R", 0, 0, 0], ["D", -1], ["Q", -1, 1], ["T", 1, 1], ["R", 0, 0, 2], ["Z", -2], ["G", 1, 1], ["R", 0, 0, 1], ["W", 2, 0], ["A", -2], ["I", -3], ["R", 0, 0, 3], ["L", 0, 1], ["M", -1], ["R", 0, 1, 0], ["R", 0, 1, 1], ["R", 0, 1, 3], ["R", 0, 1, 2], ["V", 0, 0], ["B", -1], ["W", 2, 1], ["X", 1], ["F", -3], ["Q", 0, 0], ["E", -2]]:
+        for i in range(chunks + 6):
+            for name, off, *a in [["G", 1, 0], ["G", 1, 1], ["W", 2, 0], ["W", 2, 1], ["L", 0, 0], ["A", -3], ["R", 0, 0, 0], ["I", -4], ["R", 0, 0, 2], ["D", -2], ["R", 0, 0, 3], ["B", -2], ["P", -1, 0], ["L", 0, 1], ["T", 2, 0], ["R", 0, 1, 0], ["R", 0, 0, 1], ["R", 0, 1, 2], ["V", -1, 0], ["R", 0, 1, 3], ["V", -1, 1], ["T", 2, 1], ["Z", -2], ["X", 1], ["R", 0, 1, 1], ["Q", -1, 0], ["P", -1, 1], ["Q", -1, 1], ["E", -3], ["F", -4], ["M", -1]]:
                 if (name, i + off) + tuple(a) not in done:
                     do(name, i + off, *a)

@@ -1,6 +1,7 @@
+from contextlib import ExitStack
+
 import concourse.mybir as mybir
 from concourse.masks import make_identity
-from contextlib import ExitStack
 
 F32 = mybir.dt.float32
 BF16 = mybir.dt.bfloat16
@@ -18,46 +19,57 @@ TOKENS = B * S
 FLOPS = 2 * TOKENS * K1 * K2 + 2 * TOKENS * K2 * N
 
 P = 128
+PACK = 4
+GROUPS = K2 // (P * PACK)
 ROWS = TOKENS // P
-SIZES = [1, 2] + [4] * 11 + [2, 1]
-DIRECT = [2, 4, 5, 7, 8, 10, 11]
-POOL = [224, 224]
+WIDE = 4
+SIZES = [1, 2] + [WIDE] * 11 + [2, 1]
+CHUNKS = len(SIZES)
+FIRST = [sum(SIZES[:c]) for c in range(CHUNKS)]
+
+
+def rows_of(c):
+    return SIZES[c] if 0 <= c < CHUNKS else 0
+
+
+def bias_on_vector(c):
+    return SIZES[c] == WIDE and c % 3 != 0
+
+
+def woven_on_gpsimd(c, g):
+    return SIZES[c] == WIDE and g == 0
 
 
 def tile_resourceallocationnetwork_pa_t_w8_kernel(
     tc, g1_bytes, g1_scale, iab, sW2_words, sW2_scales, sb2, sW3_words, sW3_scales, sb3, out
 ):
     nc = tc.nc
-    chunks = len(SIZES)
-    first = [sum(SIZES[:c]) for c in range(chunks)]
-    g1_v = g1_bytes.rearrange("b s k -> (b s) k").rearrange("(p j) k -> p j k", j=ROWS)
-    out_v = out.rearrange("b s n -> (b s) n").rearrange("(p j) n -> p j n", j=ROWS)
+    g1_rows = g1_bytes.rearrange("b s k -> (b s) k").rearrange("(p j) k -> p j k", j=ROWS)
+    out_rows = out.rearrange("b s n -> (b s) n").rearrange("(p j) n -> p j n", j=ROWS)
 
     with ExitStack() as ctx:
         keep = ctx.enter_context(tc.tile_pool(name="keep", bufs=1))
         two = ctx.enter_context(tc.tile_pool(name="two", bufs=2))
         three = ctx.enter_context(tc.tile_pool(name="three", bufs=3))
-        five = ctx.enter_context(tc.tile_pool(name="five", bufs=5))
         four = ctx.enter_context(tc.tile_pool(name="four", bufs=4))
-        turn_ps = ctx.enter_context(tc.psum_pool(name="turn_ps", bufs=2))
-        h_ps = ctx.enter_context(tc.psum_pool(name="h_ps", bufs=4))
-        zt_ps = ctx.enter_context(tc.psum_pool(name="zt_ps", bufs=1))
-        z_ps = ctx.enter_context(tc.psum_pool(name="z_ps", bufs=1))
+        five = ctx.enter_context(tc.tile_pool(name="five", bufs=5))
+        x_banks = ctx.enter_context(tc.psum_pool(name="x_banks", bufs=2))
+        h_banks = ctx.enter_context(tc.psum_pool(name="h_banks", bufs=4))
+        y_bank = ctx.enter_context(tc.psum_pool(name="y_bank", bufs=1))
+        z_bank = ctx.enter_context(tc.psum_pool(name="z_bank", bufs=1))
 
-        raw = [
-            keep.tile([P, SIZES[c], K1], U8, name="raw_%d" % c, align_bytes=64) for c in range(chunks)
-        ]
-        scale = keep.tile([P, 4], F32, name="scale")
+        raw = [keep.tile([P, SIZES[c], K1], U8, name="raw_%d" % c, align_bytes=64) for c in range(CHUNKS)]
+        scale = keep.tile([P, PACK], F32, name="scale")
         w2_raw = keep.tile([P, K2], I32, name="w2_raw", align_bytes=64)
-        w2 = keep.tile([P, 2, 4, P], I32, name="w2", align_bytes=64)
         w2s_raw = keep.tile([P, K2], U8, name="w2s_raw", align_bytes=64)
-        w2s = keep.tile([P, 2, 4, P], U8, name="w2s", align_bytes=64)
-        w3 = keep.tile([P, 2, N], I32, name="w3", align_bytes=64)
-        w3s = keep.tile([P, 2, N], U8, name="w3s", align_bytes=64)
-        b2 = keep.tile([P, 2, 4], BF16, name="b2")
-        b3 = keep.tile([P, 1], BF16, name="b3")
+        w2 = keep.tile([P, GROUPS, PACK, P], I32, name="w2", align_bytes=64)
+        w2s = keep.tile([P, GROUPS, PACK, P], U8, name="w2s", align_bytes=64)
+        w3 = keep.tile([P, GROUPS, N], I32, name="w3", align_bytes=64)
+        w3s = keep.tile([P, GROUPS, N], U8, name="w3s", align_bytes=64)
+        b2 = keep.tile([P, GROUPS, PACK], BF16, name="b2")
+        b3_column = keep.tile([P, 1], BF16, name="b3_column")
         b3_row = keep.tile([P, N], BF16, name="b3_row")
-        b3_rows = keep.tile([P, 4, N], F32, name="b3_rows")
+        b3_rows = keep.tile([P, WIDE, N], F32, name="b3_rows")
         iab_raw = keep.tile([P, ROWS], BF16, name="iab_raw")
         share = keep.tile([P, ROWS], F32, name="share")
         ident = keep.tile([P, P], F32, name="ident", align_bytes=64)
@@ -65,366 +77,316 @@ def tile_resourceallocationnetwork_pa_t_w8_kernel(
 
         ctx.enter_context(tc.manual_schedule())
 
-        def load(c):
-            nc.sync.dma_start(out=raw[c][:], in_=g1_v[:, first[c] : first[c] + SIZES[c], :])
-
         nc.vector.memset(w2s_raw[:].bitcast(I32), 0)
         nc.vector.memset(w3s[:].rearrange("p g n -> p (g n)").bitcast(I32), 0)
         nc.vector.memset(warm[:], 0.0)
         nc.scalar.activation(out=warm[:], in_=warm[:], func=ACT.Exp)
         make_identity(nc, ident[:])
 
+        def load(c):
+            nc.sync.dma_start(out=raw[c][:], in_=g1_rows[:, FIRST[c] : FIRST[c] + SIZES[c], :])
+
         load(0)
-        nc.sync.dma_start(out=scale[:], in_=g1_scale.rearrange("a b (p t) -> p (a b t)", t=4))
-        load(1)
-        nc.sync.dma_start(
-            out=w2_raw[:], in_=sW2_words[0].rearrange("p n t -> p (n t)").bitcast(I32)
-        )
         for q in range(4):
             nc.sync.dma_start(
                 out=w2s_raw[32 * q : 32 * q + 4, :].bitcast(I32),
                 in_=sW2_scales[0, 4 * q : 4 * q + 4, :].bitcast(I32),
             )
-        nc.gpsimd.dma_start(out=b2[:], in_=sb2.rearrange("(g p t) -> p g t", p=P, t=4))
+        nc.sync.dma_start(out=scale[:], in_=g1_scale.rearrange("a b (p t) -> p (a b t)", t=PACK))
+        load(1)
+        nc.sync.dma_start(out=w2_raw[:], in_=sW2_words[0].rearrange("p n t -> p (n t)").bitcast(I32))
+        nc.gpsimd.dma_start(out=b2[:], in_=sb2.rearrange("(g p t) -> p g t", p=P, t=PACK))
         nc.gpsimd.dma_start(out=b3_row[:], in_=sb3.partition_broadcast(P))
-        nc.gpsimd.dma_start(out=b3[:], in_=sb3.rearrange("(n o) -> n o", o=1))
+        nc.gpsimd.dma_start(out=b3_column[:], in_=sb3.rearrange("(n o) -> n o", o=1))
         nc.gpsimd.dma_start(
             out=iab_raw[:], in_=iab.rearrange("b s -> (b s)").rearrange("(p j) -> p j", j=ROWS)
         )
         load(2)
-        for g in range(2):
-            nc.sync.dma_start(
-                out=w3[:, g, :], in_=sW3_words[g].rearrange("p n t -> p (n t)").bitcast(I32)
-            )
+        for g in range(GROUPS):
+            nc.sync.dma_start(out=w3[:, g, :], in_=sW3_words[g].rearrange("p n t -> p (n t)").bitcast(I32))
         for q in range(4):
             nc.sync.dma_start(
-                out=w3s[32 * q : 32 * q + 4, :, :].rearrange("p g n -> p g n").bitcast(I32),
+                out=w3s[32 * q : 32 * q + 4, :, :].bitcast(I32),
                 in_=sW3_scales[:, 4 * q : 4 * q + 4, :].rearrange("g q n -> q g n").bitcast(I32),
             )
-        for c in range(3, chunks):
+        for c in range(3, CHUNKS):
             load(c)
-
 
         live = {}
 
+        def sort_scales(g):
+            nc.vector.tensor_copy(
+                out=w2s[:, g, :, :],
+                in_=w2s_raw[:, PACK * P * g : PACK * P * (g + 1)].rearrange("p (m t) -> p t m", t=PACK),
+            )
+
+        def sort_words(g):
+            nc.vector.tensor_copy(
+                out=w2[:, g, :, :],
+                in_=w2_raw[:, PACK * P * g : PACK * P * (g + 1)].rearrange("p (m t) -> p t m", t=PACK),
+            )
+
         def widen(c, half):
-            n = SIZES[c]
-            if half == 0:
-                live["x", c] = three.tile([P, 4, K1], BF16, name="x", align_bytes=64)
-            x = live["x", c]
+            n = rows_of(c)
             lo, hi = (half * n + 1) // 2, ((half + 1) * n + 1) // 2
-            if lo < hi:
-                nc.scalar.copy(out=x[:, lo:hi, :], in_=raw[c][:, lo:hi, :].bitcast(FP8))
+            if lo == hi:
+                return
+            if half == 0:
+                live["x", c] = three.tile([P, WIDE, K1], BF16, name="x", align_bytes=64)
+            nc.scalar.copy(out=live["x", c][:, lo:hi, :], in_=raw[c][:, lo:hi, :].bitcast(FP8))
 
-        def turn(c, b):
-            x = live["x", c]
-            xt = turn_ps.tile([P, 2, 2, P], F32, name="xt")
-            for a in range(min(2, SIZES[c] - 2 * b)):
-                words = x[:, 2 * b + a, :].bitcast(F32)
+        def turn(c, half):
+            rows = min(2, rows_of(c) - 2 * half)
+            if rows <= 0:
+                return
+            turned = x_banks.tile([P, 2, 2, P], F32, name="turned")
+            live["turned", c, half] = turned
+            for a in range(rows):
+                words = live["x", c][:, 2 * half + a, :].bitcast(F32)
                 for u in range(2):
-                    nc.tensor.transpose(xt[:, u, a, :], words[:, u : 2 * P : 2], ident[:])
-            live["turned", c, b] = xt
+                    nc.tensor.transpose(turned[:, u, a, :], words[:, u : 2 * P : 2], ident[:])
 
-        def gather(c, b):
-            m = min(2, SIZES[c] - 2 * b)
-            if b == 0:
-                live["xg", c] = two.tile([P, 4 * P, 4], BF16, name="xg", align_bytes=64)
-            xg = live["xg", c]
-            xt = live["turned", c, b]
+        def scale_x(c, half):
+            rows = min(2, rows_of(c) - 2 * half)
+            if rows <= 0:
+                return
+            if half == 0:
+                live["xg", c] = two.tile([P, WIDE * P, PACK], BF16, name="xg", align_bytes=64)
+            start = 2 * P * half
             nc.vector.tensor_tensor(
-                out=xg[:, 2 * P * b : 2 * P * b + m * P, :].rearrange("p n (u e) -> p n u e", e=2),
-                in0=xt[:]
+                out=live["xg", c][:, start : start + rows * P, :].rearrange("p n (u e) -> p n u e", e=2),
+                in0=live["turned", c, half][:]
                 .rearrange("p u a r -> p u (a r)")
-                .bitcast(BF16)[:, :, : 2 * P * m]
+                .bitcast(BF16)[:, :, : 2 * P * rows]
                 .rearrange("p u (n e) -> p n u e", e=2),
-                in1=scale[:]
-                .rearrange("p (o u e) -> p o u e", o=1, e=2)
-                .to_broadcast([P, m * P, 2, 2]),
+                in1=scale[:].rearrange("p (o u e) -> p o u e", o=1, e=2).to_broadcast([P, rows * P, 2, 2]),
                 op=ALU.mult,
             )
 
-        def quant_x(c):
-            n = SIZES[c]
-            codes = two.tile([P, 4 * P], U32, name="x_codes", align_bytes=64)
-            scales = two.tile([P, 4 * P], U8, name="x_scales", align_bytes=64)
+        def quantise_x(c):
+            n = P * rows_of(c)
+            if n == 0:
+                return
+            codes = two.tile([P, WIDE * P], U32, name="x_codes", align_bytes=64)
+            scales = two.tile([P, WIDE * P], U8, name="x_scales", align_bytes=64)
             live["xq", c] = (codes, scales)
             nc.vector.quantize_mx(
-                out=codes[:, : n * P].bitcast(FP8X4),
-                scales=scales[:, : n * P],
-                in_=live["xg", c][:, : n * P, :].rearrange("p n t -> p (n t)"),
+                out=codes[:, :n].bitcast(FP8X4),
+                scales=scales[:, :n],
+                in_=live["xg", c][:, :n, :].rearrange("p n t -> p (n t)"),
             )
 
         def layer1(c, g):
-            w = SIZES[c] * P
+            n = P * rows_of(c)
+            if n == 0:
+                return
             codes, scales = live["xq", c]
-            live["h", c, g] = []
-            for t in range(4):
-                acc = h_ps.tile([P, 4 * P], F32, name="acc")
+            for t in range(PACK):
+                sums = h_banks.tile([P, WIDE * P], F32, name="sums")
+                live["sums", c, g, t] = sums
                 nc.tensor.matmul_mx(
-                    out=acc[:, :w],
+                    out=sums[:, :n],
                     lhsT=w2[:, g, t, :].bitcast(FP8X4),
                     lhsT_scale=w2s[:, g, t, :],
-                    rhs=codes[:, :w].bitcast(FP8X4),
-                    rhs_scale=scales[:, :w],
+                    rhs=codes[:, :n].bitcast(FP8X4),
+                    rhs_scale=scales[:, :n],
                     start=True,
                     stop=True,
                 )
-                live["h", c, g].append(acc)
 
-        def relu(c, g, planes):
-            w = SIZES[c] * P
-            if planes[0] == 0:
-                live["hp", c, g] = five.tile([P, 4, 4 * P], BF16, name="hp", align_bytes=64)
-            hp = live["hp", c, g]
-            for t in planes:
+        def relu(c, g):
+            n = P * rows_of(c)
+            if n == 0:
+                return
+            planes = five.tile([P, PACK, WIDE * P], BF16, name="planes", align_bytes=64)
+            live["planes", c, g] = planes
+            for t in range(PACK):
                 nc.scalar.activation(
-                    out=hp[:, t, :w],
-                    in_=live["h", c, g][t][:, :w],
-                    func=ACT.Relu,
-                    bias=b2[:, g, t : t + 1],
+                    out=planes[:, t, :n], in_=live["sums", c, g, t][:, :n], func=ACT.Relu, bias=b2[:, g, t : t + 1]
                 )
-
-        def pooled(c, g):
-            return POOL[g] if SIZES[c] == 4 and c >= 2 else 0
-
-        def tile_hg(c, g):
-            if ("hg", c, g) not in live:
-                live["hg", c, g] = two.tile([P, 4 * P, 4], BF16, name="hg", align_bytes=64)
-            return live["hg", c, g]
 
         def weave(c, g):
-            w = SIZES[c] * P
-            hg = tile_hg(c, g)
-            w -= pooled(c, g)
-            if w:
-                nc.vector.tensor_copy(
-                    out=hg[:, :w, :].rearrange("p (c i) t -> p c t i", i=4),
-                    in_=live["hp", c, g][:, :, :w].rearrange("p t (c i) -> p c t i", i=4),
-                )
-
-        def pool_weave(c, g):
-            w = SIZES[c] * P
-            k = pooled(c, g)
-            if k:
-                hg = tile_hg(c, g)
+            n = P * rows_of(c)
+            if n == 0:
+                return
+            woven = two.tile([P, WIDE * P, PACK], BF16, name="woven", align_bytes=64)
+            live["woven", c, g] = woven
+            planes = live["planes", c, g]
+            if woven_on_gpsimd(c, g):
                 nc.gpsimd.tensor_scalar(
-                    out=hg[:, w - k : w, :],
-                    in0=live["hp", c, g][:, :, w - k : w].rearrange("p t n -> p n t"),
+                    out=woven[:, :n, :],
+                    in0=planes[:, :, :n].rearrange("p t n -> p n t"),
                     scalar1=1.0,
                     scalar2=0.0,
                     op0=ALU.mult,
                     op1=ALU.add,
                 )
+            else:
+                nc.vector.tensor_copy(
+                    out=woven[:, :n, :].rearrange("p (c i) t -> p c t i", i=4),
+                    in_=planes[:, :, :n].rearrange("p t (c i) -> p c t i", i=4),
+                )
 
-        def quant_h(c, g):
-            w = SIZES[c] * P
-            codes = four.tile([P, 4 * P], U32, name="h_codes", align_bytes=64)
-            scales = four.tile([P, 4 * P], U8, name="h_scales", align_bytes=64)
+        def quantise_h(c, g):
+            n = P * rows_of(c)
+            if n == 0:
+                return
+            codes = four.tile([P, WIDE * P], U32, name="h_codes", align_bytes=64)
+            scales = four.tile([P, WIDE * P], U8, name="h_scales", align_bytes=64)
             live["hq", c, g] = (codes, scales)
             nc.vector.quantize_mx(
-                out=codes[:, :w].bitcast(FP8X4),
-                scales=scales[:, :w],
-                in_=live["hg", c, g][:, :w, :].rearrange("p n t -> p (n t)"),
+                out=codes[:, :n].bitcast(FP8X4),
+                scales=scales[:, :n],
+                in_=live["woven", c, g][:, :n, :].rearrange("p n t -> p (n t)"),
             )
 
         def layer2(c):
-            w = SIZES[c] * P
-            if c in DIRECT:
-                z = zt_ps.tile([P, 4 * P], F32, name="zt").rearrange("p (a n) -> p a n", a=4)
-                live["zt", c] = z
-                for a in range(SIZES[c]):
-                    cols = slice(a * P, (a + 1) * P)
-                    for g in range(2):
-                        codes, scales = live["hq", c, g]
-                        nc.tensor.matmul_mx(
-                            out=z[:, a, :],
-                            lhsT=codes[:, cols].bitcast(FP8X4),
-                            lhsT_scale=scales[:, cols],
-                            rhs=w3[:, g, :].bitcast(FP8X4),
-                            rhs_scale=w3s[:, g, :],
-                            start=(g == 0),
-                            stop=(g == 1),
-                        )
+            n = P * rows_of(c)
+            if n == 0:
                 return
-            zt = zt_ps.tile([P, 4 * P], F32, name="zt")
-            live["zt", c] = zt
-            for g in range(2):
-                codes, scales = live["hq", c, g]
-                nc.tensor.matmul_mx(
-                    out=zt[:, :w],
-                    lhsT=w3[:, g, :].bitcast(FP8X4),
-                    lhsT_scale=w3s[:, g, :],
-                    rhs=codes[:, :w].bitcast(FP8X4),
-                    rhs_scale=scales[:, :w],
-                    start=(g == 0),
-                    stop=(g == 1),
-                )
+            y = y_bank.tile([P, WIDE * P], F32, name="y")
+            live["y", c] = y
+            for lo in range(0, n, P) if bias_on_vector(c) else [0]:
+                for g in range(GROUPS):
+                    codes, scales = live["hq", c, g]
+                    hi = lo + P if bias_on_vector(c) else n
+                    h_codes, h_scales = codes[:, lo:hi].bitcast(FP8X4), scales[:, lo:hi]
+                    w_codes, w_scales = w3[:, g, :].bitcast(FP8X4), w3s[:, g, :]
+                    swap = bias_on_vector(c)
+                    nc.tensor.matmul_mx(
+                        out=y[:, lo:hi],
+                        lhsT=h_codes if swap else w_codes,
+                        lhsT_scale=h_scales if swap else w_scales,
+                        rhs=w_codes if swap else h_codes,
+                        rhs_scale=w_scales if swap else h_scales,
+                        start=(g == 0),
+                        stop=(g == GROUPS - 1),
+                    )
 
-        def add_b3(c):
-            w = SIZES[c] * P
-            if c in DIRECT:
-                n = SIZES[c]
-                zb = four.tile([P, 4, N], F32, name="zb")
-                live["zb", c] = zb
-                nc.vector.tensor_tensor(
-                    out=zb[:, :n, :], in0=live["zt", c][:, :n, :], in1=b3_rows[:, :n, :], op=ALU.add
-                )
+        def add_b3_on_scalar(c):
+            n = P * rows_of(c)
+            if n == 0 or bias_on_vector(c):
                 return
-            zs = four.tile([P, 4 * P], F32, name="zs")
-            live["zs", c] = zs
-            nc.scalar.activation(
-                out=zs[:, :w], in_=live["zt", c][:, :w], func=ACT.Identity, bias=b3[:]
-            )
+            zt = four.tile([P, WIDE * P], F32, name="zt")
+            live["zt", c] = zt
+            nc.scalar.activation(out=zt[:, :n], in_=live["y", c][:, :n], func=ACT.Identity, bias=b3_column[:])
 
         def turn_z(c):
-            if c in DIRECT:
+            if rows_of(c) == 0 or bias_on_vector(c):
                 return
-            z = z_ps.tile([P, 4, N], F32, name="z")
-            live["zb", c] = z
-            for a in range(SIZES[c]):
-                nc.tensor.transpose(z[:, a, :], live["zs", c][:, a * P : (a + 1) * P], ident[:])
+            z = z_bank.tile([P, WIDE, N], F32, name="z")
+            live["z", c] = z
+            for a in range(rows_of(c)):
+                nc.tensor.transpose(z[:, a, :], live["zt", c][:, a * P : (a + 1) * P], ident[:])
 
-        def row_max(c):
-            n = SIZES[c]
-            nm = four.tile([P, 4], F32, name="nm")
-            live["nm", c] = nm
-            nc.vector.tensor_reduce(
-                out=nm[:, :n], in_=live["zb", c][:, :n, :], axis=AX.X, op=ALU.max, negate=True
+        def add_b3_on_vector(c):
+            n = rows_of(c)
+            if n == 0 or not bias_on_vector(c):
+                return
+            z = four.tile([P, WIDE, N], F32, name="z_sum")
+            live["z", c] = z
+            nc.vector.tensor_tensor(
+                out=z[:, :n, :],
+                in0=live["y", c][:].rearrange("p (a n) -> p a n", a=WIDE)[:, :n, :],
+                in1=b3_rows[:, :n, :],
+                op=ALU.add,
             )
 
-        def expo(c):
-            e = four.tile([P, 4, N], F32, name="e")
-            total = four.tile([P, 4], F32, name="total")
+        def row_max(c):
+            n = rows_of(c)
+            if n == 0:
+                return
+            top = four.tile([P, WIDE], F32, name="top")
+            live["top", c] = top
+            nc.vector.tensor_reduce(out=top[:, :n], in_=live["z", c][:, :n, :], axis=AX.X, op=ALU.max, negate=True)
+
+        def exponentials(c):
+            n = rows_of(c)
+            if n == 0:
+                return
+            e = four.tile([P, WIDE, N], F32, name="e")
+            total = four.tile([P, WIDE], F32, name="total")
             live["e", c] = (e, total)
-            for a in range(SIZES[c]):
+            for a in range(n):
                 nc.scalar.activation(
                     out=e[:, a, :],
-                    in_=live["zb", c][:, a, :],
+                    in_=live["z", c][:, a, :],
                     func=ACT.Exp,
-                    bias=live["nm", c][:, a : a + 1],
+                    bias=live["top", c][:, a : a + 1],
                     accum_out=total[:, a : a + 1],
                 )
 
         def invert(c):
-            n = SIZES[c]
-            e, total = live["e", c]
-            inv = four.tile([P, 4], F32, name="inv")
-            live["inv", c] = inv
-            nc.vector.reciprocal(out=inv[:, :n], in_=total[:, :n])
+            n = rows_of(c)
+            if n == 0:
+                return
+            inverse = four.tile([P, WIDE], F32, name="inverse")
+            live["inverse", c] = inverse
+            nc.vector.reciprocal(out=inverse[:, :n], in_=live["e", c][1][:, :n])
 
         def finish(c):
-            n = SIZES[c]
-            e, total = live["e", c]
-            res = three.tile([P, 4, N], F32, name="res")
+            n = rows_of(c)
+            if n == 0:
+                return
+            result = three.tile([P, WIDE, N], F32, name="result")
             for a in range(n):
-                j = first[c] + a
+                j = FIRST[c] + a
                 nc.vector.tensor_scalar(
-                    out=res[:, a, :],
-                    in0=e[:, a, :],
-                    scalar1=live["inv", c][:, a : a + 1],
+                    out=result[:, a, :],
+                    in0=live["e", c][0][:, a, :],
+                    scalar1=live["inverse", c][:, a : a + 1],
                     scalar2=share[:, j : j + 1],
                     op0=ALU.mult,
                     op1=ALU.mult,
                 )
-            nc.sync.dma_start(out=out_v[:, first[c] : first[c] + n, :], in_=res[:, :n, :])
+            nc.sync.dma_start(out=out_rows[:, FIRST[c] : FIRST[c] + n, :], in_=result[:, :n, :])
 
-        def on(c):
-            return 0 <= c < chunks
-
-        done = {}
-
-        def need(*keys):
-            for k in keys:
-                assert k in done, k
-
-        def mark(k):
-            done[k] = True
-
-        def do(name, c, *a):
-            if not on(c):
-                return
-            if name == "W":
-                widen(c, a[0])
-            elif name == "T":
-                if 2 * a[0] >= SIZES[c]:
-                    mark((name, c) + tuple(a))
-                    return
-                need(("W", c, 0), ("W", c, 1))
-                turn(c, a[0])
-            elif name == "G":
-                if 2 * a[0] >= SIZES[c]:
-                    mark((name, c) + tuple(a))
-                    return
-                need(("T", c, a[0]))
-                gather(c, a[0])
-            elif name == "X":
-                need(("G", c, 0), ("G", c, 1))
-                quant_x(c)
-            elif name == "L":
-                need(("X", c), ("p", 0, a[0]), ("q", 0, a[0]))
-                layer1(c, a[0])
-            elif name == "R":
-                need(("L", c, a[0]))
-                relu(c, a[0], [a[1]])
-            elif name == "V":
-                need(*[("R", c, a[0], t) for t in range(4)])
-                weave(c, a[0])
-            elif name == "P":
-                need(*[("R", c, a[0], t) for t in range(4)])
-                pool_weave(c, a[0])
-            elif name == "Q":
-                need(("V", c, a[0]), ("P", c, a[0]))
-                quant_h(c, a[0])
-            elif name == "M":
-                need(("Q", c, 0), ("Q", c, 1))
-                layer2(c)
-            elif name == "D":
-                if c not in DIRECT:
-                    return
-                need(("M", c))
-                add_b3(c)
-                mark(("B", c))
-                mark(("Z", c))
-            elif name in ("B", "Z") and c in DIRECT:
-                return
-            elif name == "p":
-                g = a[0]
-                nc.vector.tensor_copy(
-                    out=w2[:, g, :, :],
-                    in_=w2_raw[:, 4 * P * g : 4 * P * (g + 1)].rearrange("p (m t) -> p t m", t=4),
-                )
-            elif name == "q":
-                g = a[0]
-                (nc.vector if g == 0 else nc.gpsimd).tensor_copy(
-                    out=w2s[:, g, :, :],
-                    in_=w2s_raw[:, 4 * P * g : 4 * P * (g + 1)].rearrange("p (m t) -> p t m", t=4),
-                )
-            elif name == "B":
-                need(("M", c))
-                add_b3(c)
-            elif name == "Z":
-                need(("B", c))
-                turn_z(c)
-            elif name == "A":
-                need(("Z", c))
-                row_max(c)
-            elif name == "E":
-                need(("A", c))
-                expo(c)
-            elif name == "I":
-                need(("E", c))
-                invert(c)
-            elif name == "F":
-                need(("I", c))
-                finish(c)
-            mark((name, c) + tuple(a))
-
-        for name, c, *a in [["W", 0, 0], ["G", 0, 1], ["W", 1, 0], ["W", 0, 1], ["T", 0, 0], ["W", 1, 1], ["G", 0, 0], ["W", 2, 0], ["p", 0, 0], ["X", 0], ["T", 1, 0], ["q", 0, 0], ["G", 1, 0], ["p", 0, 1], ["q", 0, 1], ["G", 1, 1], ["T", 0, 1], ["L", 0, 0], ["W", 2, 1], ["X", 1], ["R", 0, 0, 0], ["R", 0, 0, 2], ["R", 0, 0, 3], ["R", 0, 0, 1], ["L", 0, 1], ["R", 0, 1, 0], ["T", 1, 1], ["R", 0, 1, 1], ["R", 0, 1, 2], ["R", 0, 1, 3]]:
-            do(name, c, *a)
+        widen(0, 0)
+        widen(1, 0)
+        widen(1, 1)
+        widen(2, 0)
+        sort_scales(0)
+        sort_scales(1)
+        turn(0, 0)
+        scale_x(0, 0)
+        turn(1, 0)
+        sort_words(0)
+        quantise_x(0)
+        layer1(0, 0)
+        relu(0, 0)
+        widen(2, 1)
+        sort_words(1)
+        layer1(0, 1)
+        relu(0, 1)
+        scale_x(1, 0)
+        quantise_x(1)
+        turn(2, 0)
+        turn(2, 1)
         nc.gpsimd.tensor_copy(out=share[:], in_=iab_raw[:])
-        for a in range(4):
+        for a in range(WIDE):
             nc.gpsimd.tensor_copy(out=b3_rows[:, a, :], in_=b3_row[:])
-        for i in range(chunks + 6):
-            for name, off, *a in [["G", 1, 0], ["G", 1, 1], ["W", 2, 0], ["W", 2, 1], ["L", 0, 0], ["A", -3], ["R", 0, 0, 0], ["I", -4], ["R", 0, 0, 2], ["D", -2], ["R", 0, 0, 3], ["B", -2], ["P", -1, 0], ["L", 0, 1], ["T", 2, 0], ["R", 0, 1, 0], ["R", 0, 0, 1], ["R", 0, 1, 2], ["V", -1, 0], ["R", 0, 1, 3], ["V", -1, 1], ["T", 2, 1], ["Z", -2], ["X", 1], ["R", 0, 1, 1], ["Q", -1, 0], ["P", -1, 1], ["Q", -1, 1], ["E", -3], ["F", -4], ["M", -1]]:
-                if (name, i + off) + tuple(a) not in done:
-                    do(name, i + off, *a)
+
+        for i in range(1, CHUNKS + 5):
+            widen(i + 2, 0)
+            widen(i + 2, 1)
+            add_b3_on_scalar(i - 2)
+            scale_x(i + 1, 0)
+            row_max(i - 3)
+            add_b3_on_vector(i - 2)
+            invert(i - 4)
+            layer1(i, 0)
+            turn(i + 2, 0)
+            relu(i, 0)
+            layer1(i, 1)
+            weave(i - 1, 0)
+            scale_x(i + 1, 1)
+            exponentials(i - 3)
+            relu(i, 1)
+            finish(i - 4)
+            weave(i - 1, 1)
+            turn_z(i - 2)
+            quantise_h(i - 1, 0)
+            quantise_h(i - 1, 1)
+            layer2(i - 1)
+            quantise_x(i + 1)
+            turn(i + 2, 1)

@@ -214,8 +214,8 @@ def tile_resourceallocationnetwork_pa_t_w8_kernel(
             planes = live["planes", c, g]
             if woven_on_gpsimd(c, g):
                 nc.gpsimd.tensor_scalar(
-                    out=woven[:, :n, :],
-                    in0=planes[:, :, :n].rearrange("p t n -> p n t"),
+                    out=woven[:, :n, :].rearrange("p (c i) t -> p c t i", i=4),
+                    in0=planes[:, :, :n].rearrange("p t (c i) -> p c t i", i=4),
                     scalar1=1.0,
                     scalar2=0.0,
                     op0=ALU.mult,

from contextlib import ExitStack

import concourse.mybir as mybir
from concourse.masks import make_identity

F32 = mybir.dt.float32
BF16 = mybir.dt.bfloat16
I32 = mybir.dt.int32
U32 = mybir.dt.uint32
U8 = mybir.dt.uint8
FP8 = mybir.dt.float8_e4m3fn
FP8X4 = mybir.dt.float8_e4m3fn_x4
ACT = mybir.ActivationFunctionType
ALU = mybir.AluOpType
AX = mybir.AxisListType

B, S, K1, K2, N = 640, 10, 512, 1024, 128
TOKENS = B * S
FLOPS = 2 * TOKENS * K1 * K2 + 2 * TOKENS * K2 * N

P = 128
PACK = 4
GROUPS = K2 // (P * PACK)
ROWS = TOKENS // P
WIDE = 4
SIZES = [1, 2] + [WIDE] * 11 + [2, 1]
CHUNKS = len(SIZES)
FIRST = [sum(SIZES[:c]) for c in range(CHUNKS)]


def rows_of(c):
    return SIZES[c] if 0 <= c < CHUNKS else 0


def bias_on_vector(c):
    return SIZES[c] == WIDE and c % 3 != 0


def woven_on_gpsimd(c, g):
    return SIZES[c] == WIDE and g == 0


def tile_resourceallocationnetwork_pa_t_w8_kernel(
    tc, g1_bytes, g1_scale, iab, sW2_words, sW2_scales, sb2, sW3_words, sW3_scales, sb3, out
):
    nc = tc.nc
    g1_rows = g1_bytes.rearrange("b s k -> (b s) k").rearrange("(p j) k -> p j k", j=ROWS)
    out_rows = out.rearrange("b s n -> (b s) n").rearrange("(p j) n -> p j n", j=ROWS)

    with ExitStack() as ctx:
        keep = ctx.enter_context(tc.tile_pool(name="keep", bufs=1))
        two = ctx.enter_context(tc.tile_pool(name="two", bufs=2))
        three = ctx.enter_context(tc.tile_pool(name="three", bufs=3))
        four = ctx.enter_context(tc.tile_pool(name="four", bufs=4))
        five = ctx.enter_context(tc.tile_pool(name="five", bufs=5))
        x_banks = ctx.enter_context(tc.psum_pool(name="x_banks", bufs=2))
        h_banks = ctx.enter_context(tc.psum_pool(name="h_banks", bufs=4))
        y_bank = ctx.enter_context(tc.psum_pool(name="y_bank", bufs=1))
        z_bank = ctx.enter_context(tc.psum_pool(name="z_bank", bufs=1))

        raw = [keep.tile([P, SIZES[c], K1], U8, name="raw_%d" % c, align_bytes=64) for c in range(CHUNKS)]
        scale = keep.tile([P, PACK], F32, name="scale")
        w2_raw = keep.tile([P, K2], I32, name="w2_raw", align_bytes=64)
        w2s_raw = keep.tile([P, K2], U8, name="w2s_raw", align_bytes=64)
        w2 = keep.tile([P, GROUPS, PACK, P], I32, name="w2", align_bytes=64)
        w2s = keep.tile([P, GROUPS, PACK, P], U8, name="w2s", align_bytes=64)
        w3 = keep.tile([P, GROUPS, N], I32, name="w3", align_bytes=64)
        w3s = keep.tile([P, GROUPS, N], U8, name="w3s", align_bytes=64)
        b2 = keep.tile([P, GROUPS, PACK], BF16, name="b2")
        b3_column = keep.tile([P, 1], BF16, name="b3_column")
        b3_row = keep.tile([P, N], BF16, name="b3_row")
        b3_rows = keep.tile([P, WIDE, N], F32, name="b3_rows")
        iab_raw = keep.tile([P, ROWS], BF16, name="iab_raw")
        share = keep.tile([P, ROWS], F32, name="share")
        ident = keep.tile([P, P], F32, name="ident", align_bytes=64)
        warm = keep.tile([P, 1], F32, name="warm")

        ctx.enter_context(tc.manual_schedule())

        nc.vector.memset(w2s_raw[:].bitcast(I32), 0)
        nc.vector.memset(w3s[:].rearrange("p g n -> p (g n)").bitcast(I32), 0)
        nc.vector.memset(warm[:], 0.0)
        nc.scalar.activation(out=warm[:], in_=warm[:], func=ACT.Exp)
        make_identity(nc, ident[:])

        def load(c):
            nc.sync.dma_start(out=raw[c][:], in_=g1_rows[:, FIRST[c] : FIRST[c] + SIZES[c], :])

        load(0)
        for q in range(4):
            nc.sync.dma_start(
                out=w2s_raw[32 * q : 32 * q + 4, :].bitcast(I32),
                in_=sW2_scales[0, 4 * q : 4 * q + 4, :].bitcast(I32),
            )
        nc.sync.dma_start(out=scale[:], in_=g1_scale.rearrange("a b (p t) -> p (a b t)", t=PACK))
        load(1)
        nc.sync.dma_start(out=w2_raw[:], in_=sW2_words[0].rearrange("p n t -> p (n t)").bitcast(I32))
        nc.gpsimd.dma_start(out=b2[:], in_=sb2.rearrange("(g p t) -> p g t", p=P, t=PACK))
        nc.gpsimd.dma_start(out=b3_row[:], in_=sb3.partition_broadcast(P))
        nc.gpsimd.dma_start(out=b3_column[:], in_=sb3.rearrange("(n o) -> n o", o=1))
        nc.gpsimd.dma_start(
            out=iab_raw[:], in_=iab.rearrange("b s -> (b s)").rearrange("(p j) -> p j", j=ROWS)
        )
        load(2)
        for g in range(GROUPS):
            nc.sync.dma_start(out=w3[:, g, :], in_=sW3_words[g].rearrange("p n t -> p (n t)").bitcast(I32))
        for q in range(4):
            nc.sync.dma_start(
                out=w3s[32 * q : 32 * q + 4, :, :].bitcast(I32),
                in_=sW3_scales[:, 4 * q : 4 * q + 4, :].rearrange("g q n -> q g n").bitcast(I32),
            )
        for c in range(3, CHUNKS):
            load(c)

        live = {}

        def sort_scales(g):
            nc.vector.tensor_copy(
                out=w2s[:, g, :, :],
                in_=w2s_raw[:, PACK * P * g : PACK * P * (g + 1)].rearrange("p (m t) -> p t m", t=PACK),
            )

        def sort_words(g):
            nc.vector.tensor_copy(
                out=w2[:, g, :, :],
                in_=w2_raw[:, PACK * P * g : PACK * P * (g + 1)].rearrange("p (m t) -> p t m", t=PACK),
            )

        def widen(c, half):
            n = rows_of(c)
            lo, hi = (half * n + 1) // 2, ((half + 1) * n + 1) // 2
            if lo == hi:
                return
            if half == 0:
                live["x", c] = three.tile([P, WIDE, K1], BF16, name="x", align_bytes=64)
            nc.scalar.copy(out=live["x", c][:, lo:hi, :], in_=raw[c][:, lo:hi, :].bitcast(FP8))

        def turn(c, half):
            rows = min(2, rows_of(c) - 2 * half)
            if rows <= 0:
                return
            turned = x_banks.tile([P, 2, 2, P], F32, name="turned")
            live["turned", c, half] = turned
            for a in range(rows):
                words = live["x", c][:, 2 * half + a, :].bitcast(F32)
                for u in range(2):
                    nc.tensor.transpose(turned[:, u, a, :], words[:, u : 2 * P : 2], ident[:])

        def scale_x(c, half):
            rows = min(2, rows_of(c) - 2 * half)
            if rows <= 0:
                return
            if half == 0:
                live["xg", c] = two.tile([P, WIDE * P, PACK], BF16, name="xg", align_bytes=64)
            start = 2 * P * half
            nc.vector.tensor_tensor(
                out=live["xg", c][:, start : start + rows * P, :].rearrange("p n (u e) -> p n u e", e=2),
                in0=live["turned", c, half][:]
                .rearrange("p u a r -> p u (a r)")
                .bitcast(BF16)[:, :, : 2 * P * rows]
                .rearrange("p u (n e) -> p n u e", e=2),
                in1=scale[:].rearrange("p (o u e) -> p o u e", o=1, e=2).to_broadcast([P, rows * P, 2, 2]),
                op=ALU.mult,
            )

        def quantise_x(c):
            n = P * rows_of(c)
            if n == 0:
                return
            codes = two.tile([P, WIDE * P], U32, name="x_codes", align_bytes=64)
            scales = two.tile([P, WIDE * P], U8, name="x_scales", align_bytes=64)
            live["xq", c] = (codes, scales)
            nc.vector.quantize_mx(
                out=codes[:, :n].bitcast(FP8X4),
                scales=scales[:, :n],
                in_=live["xg", c][:, :n, :].rearrange("p n t -> p (n t)"),
            )

        def layer1(c, g):
            n = P * rows_of(c)
            if n == 0:
                return
            codes, scales = live["xq", c]
            for t in range(PACK):
                sums = h_banks.tile([P, WIDE * P], F32, name="sums")
                live["sums", c, g, t] = sums
                nc.tensor.matmul_mx(
                    out=sums[:, :n],
                    lhsT=w2[:, g, t, :].bitcast(FP8X4),
                    lhsT_scale=w2s[:, g, t, :],
                    rhs=codes[:, :n].bitcast(FP8X4),
                    rhs_scale=scales[:, :n],
                    start=True,
                    stop=True,
                )

        def relu(c, g):
            n = P * rows_of(c)
            if n == 0:
                return
            planes = five.tile([P, PACK, WIDE * P], BF16, name="planes", align_bytes=64)
            live["planes", c, g] = planes
            for t in range(PACK):
                nc.scalar.activation(
                    out=planes[:, t, :n], in_=live["sums", c, g, t][:, :n], func=ACT.Relu, bias=b2[:, g, t : t + 1]
                )

        def weave(c, g):
            n = P * rows_of(c)
            if n == 0:
                return
            woven = two.tile([P, WIDE * P, PACK], BF16, name="woven", align_bytes=64)
            live["woven", c, g] = woven
            planes = live["planes", c, g]
            if woven_on_gpsimd(c, g):
                nc.gpsimd.tensor_scalar(
                    out=woven[:, :n, :].rearrange("p (c i) t -> p c t i", i=4),
                    in0=planes[:, :, :n].rearrange("p t (c i) -> p c t i", i=4),
                    scalar1=1.0,
                    scalar2=0.0,
                    op0=ALU.mult,
                    op1=ALU.add,
                )
            else:
                nc.vector.tensor_copy(
                    out=woven[:, :n, :].rearrange("p (c i) t -> p c t i", i=4),
                    in_=planes[:, :, :n].rearrange("p t (c i) -> p c t i", i=4),
                )

        def quantise_h(c, g):
            n = P * rows_of(c)
            if n == 0:
                return
            codes = four.tile([P, WIDE * P], U32, name="h_codes", align_bytes=64)
            scales = four.tile([P, WIDE * P], U8, name="h_scales", align_bytes=64)
            live["hq", c, g] = (codes, scales)
            nc.vector.quantize_mx(
                out=codes[:, :n].bitcast(FP8X4),
                scales=scales[:, :n],
                in_=live["woven", c, g][:, :n, :].rearrange("p n t -> p (n t)"),
            )

        def layer2(c):
            n = P * rows_of(c)
            if n == 0:
                return
            y = y_bank.tile([P, WIDE * P], F32, name="y")
            live["y", c] = y
            for lo in range(0, n, P) if bias_on_vector(c) else [0]:
                for g in range(GROUPS):
                    codes, scales = live["hq", c, g]
                    hi = lo + P if bias_on_vector(c) else n
                    h_codes, h_scales = codes[:, lo:hi].bitcast(FP8X4), scales[:, lo:hi]
                    w_codes, w_scales = w3[:, g, :].bitcast(FP8X4), w3s[:, g, :]
                    swap = bias_on_vector(c)
                    nc.tensor.matmul_mx(
                        out=y[:, lo:hi],
                        lhsT=h_codes if swap else w_codes,
                        lhsT_scale=h_scales if swap else w_scales,
                        rhs=w_codes if swap else h_codes,
                        rhs_scale=w_scales if swap else h_scales,
                        start=(g == 0),
                        stop=(g == GROUPS - 1),
                    )

        def add_b3_on_scalar(c):
            n = P * rows_of(c)
            if n == 0 or bias_on_vector(c):
                return
            zt = four.tile([P, WIDE * P], F32, name="zt")
            live["zt", c] = zt
            nc.scalar.activation(out=zt[:, :n], in_=live["y", c][:, :n], func=ACT.Identity, bias=b3_column[:])

        def turn_z(c):
            if rows_of(c) == 0 or bias_on_vector(c):
                return
            z = z_bank.tile([P, WIDE, N], F32, name="z")
            live["z", c] = z
            for a in range(rows_of(c)):
                nc.tensor.transpose(z[:, a, :], live["zt", c][:, a * P : (a + 1) * P], ident[:])

        def add_b3_on_vector(c):
            n = rows_of(c)
            if n == 0 or not bias_on_vector(c):
                return
            z = four.tile([P, WIDE, N], F32, name="z_sum")
            live["z", c] = z
            nc.vector.tensor_tensor(
                out=z[:, :n, :],
                in0=live["y", c][:].rearrange("p (a n) -> p a n", a=WIDE)[:, :n, :],
                in1=b3_rows[:, :n, :],
                op=ALU.add,
            )

        def row_max(c):
            n = rows_of(c)
            if n == 0:
                return
            top = four.tile([P, WIDE], F32, name="top")
            live["top", c] = top
            nc.vector.tensor_reduce(out=top[:, :n], in_=live["z", c][:, :n, :], axis=AX.X, op=ALU.max, negate=True)

        def exponentials(c):
            n = rows_of(c)
            if n == 0:
                return
            e = four.tile([P, WIDE, N], F32, name="e")
            total = four.tile([P, WIDE], F32, name="total")
            live["e", c] = (e, total)
            for a in range(n):
                nc.scalar.activation(
                    out=e[:, a, :],
                    in_=live["z", c][:, a, :],
                    func=ACT.Exp,
                    bias=live["top", c][:, a : a + 1],
                    accum_out=total[:, a : a + 1],
                )

        def invert(c):
            n = rows_of(c)
            if n == 0:
                return
            inverse = four.tile([P, WIDE], F32, name="inverse")
            live["inverse", c] = inverse
            nc.vector.reciprocal(out=inverse[:, :n], in_=live["e", c][1][:, :n])

        def finish(c):
            n = rows_of(c)
            if n == 0:
                return
            result = three.tile([P, WIDE, N], F32, name="result")
            for a in range(n):
                j = FIRST[c] + a
                nc.vector.tensor_scalar(
                    out=result[:, a, :],
                    in0=live["e", c][0][:, a, :],
                    scalar1=live["inverse", c][:, a : a + 1],
                    scalar2=share[:, j : j + 1],
                    op0=ALU.mult,
                    op1=ALU.mult,
                )
            nc.sync.dma_start(out=out_rows[:, FIRST[c] : FIRST[c] + n, :], in_=result[:, :n, :])

        widen(0, 0)
        widen(1, 0)
        widen(1, 1)
        widen(2, 0)
        sort_scales(0)
        sort_scales(1)
        turn(0, 0)
        scale_x(0, 0)
        turn(1, 0)
        sort_words(0)
        quantise_x(0)
        layer1(0, 0)
        relu(0, 0)
        widen(2, 1)
        sort_words(1)
        layer1(0, 1)
        relu(0, 1)
        scale_x(1, 0)
        quantise_x(1)
        turn(2, 0)
        turn(2, 1)
        nc.gpsimd.tensor_copy(out=share[:], in_=iab_raw[:])
        for a in range(WIDE):
            nc.gpsimd.tensor_copy(out=b3_rows[:, a, :], in_=b3_row[:])

        for i in range(1, CHUNKS + 5):
            widen(i + 2, 0)
            widen(i + 2, 1)
            add_b3_on_scalar(i - 2)
            scale_x(i + 1, 0)
            row_max(i - 3)
            add_b3_on_vector(i - 2)
            invert(i - 4)
            layer1(i, 0)
            turn(i + 2, 0)
            relu(i, 0)
            layer1(i, 1)
            weave(i - 1, 0)
            scale_x(i + 1, 1)
            exponentials(i - 3)
            relu(i, 1)
            finish(i - 4)
            weave(i - 1, 1)
            turn_z(i - 2)
            quantise_h(i - 1, 0)
            quantise_h(i - 1, 1)
            layer2(i - 1)
            quantise_x(i + 1)
            turn(i + 2, 1)
